import numpy as np
import ml_dtypes


def mxq(x, axis, fmt="e4m3"):
    dtype, down = {"e4m3": (ml_dtypes.float8_e4m3fn, 7), "e5m2": (ml_dtypes.float8_e5m2, 14)}[fmt]
    v = np.moveaxis(np.asarray(x, np.float32).astype(ml_dtypes.bfloat16).astype(np.float64), axis, -1)
    blocks = v.reshape(v.shape[:-1] + (-1, 32))
    amax = np.abs(blocks).max(-1, keepdims=True)
    byte = np.maximum(np.where(amax > 0, np.frexp(amax)[1] - 1 + 127, 0) - down, 1)
    scale = np.exp2(byte - 127.0)
    codes = (blocks / scale).astype(np.float32).astype(dtype).astype(np.float64)
    return np.moveaxis((codes * scale).reshape(v.shape), -1, axis)


WIDE = False


def mx_kscale(k):
    if not WIDE:
        return np.ones(k)
    levels = np.array([10, -10, 5, -5, 0])
    a = np.random.permutation(np.resize(levels, k // 512 * 4)).reshape(k // 512, 4)
    idx = np.arange(k)
    return np.exp2(a[idx // 512, idx % 128 // 32])


BF16 = ml_dtypes.bfloat16


def bf(x):
    return np.asarray(x, np.float32).astype(BF16)


def f64(x):
    return np.asarray(x).astype(np.float64)


E2M1 = np.array([0.0, 0.5, 1.0, 1.5, 2.0, 3.0, 4.0, 6.0, -0.0, -0.5, -1.0, -1.5, -2.0, -3.0, -4.0, -6.0])


def pack_weight(w, fmt):
    k, n = w.shape
    w = f64(bf(w)).reshape(k // 32, 32, n)
    amax = np.abs(w).max(1)
    if fmt == "e4m3":
        byte = np.frexp(amax)[1] - 1 + 127 - 7
    else:
        mant, ex = np.frexp(amax / 6.0)
        byte = np.where(mant > 0.5, ex, ex - 1) + 127
    byte = np.clip(np.where(amax > 0, byte, 1), 1, 254)
    scaled = (w * np.exp2(127.0 - byte)[:, None, :]).reshape(k, n).astype(np.float32)
    by_word = np.ascontiguousarray(scaled.reshape(k // 512, 128, 4, n).transpose(0, 1, 3, 2))
    if fmt == "e4m3":
        words = by_word.astype(ml_dtypes.float8_e4m3fn).view(np.uint8)
    else:
        c = by_word.astype(ml_dtypes.float4_e2m1fn).view(np.uint8) & 0xF
        words = c[..., 0::2] | (c[..., 1::2] << 4)
    return np.ascontiguousarray(words), np.ascontiguousarray(byte.astype(np.uint8).reshape(k // 512, 16, n))


def unpack_weight(words, scales, fmt):
    g, p, n, _ = words.shape
    if fmt == "e4m3":
        vals = np.ascontiguousarray(words).view(ml_dtypes.float8_e4m3fn).astype(np.float64)
    else:
        nib = np.empty((g, p, n, 4), np.uint8)
        nib[..., 0::2] = words & 0xF
        nib[..., 1::2] = words >> 4
        vals = E2M1[nib]
    vals = vals * np.repeat(np.exp2(scales.astype(np.float64) - 127.0), 8, axis=1)[..., None]
    return vals.transpose(0, 1, 3, 2).reshape(g * 512, n)


B, N, D, H, HD, FF = 2, 64, 16384, 8, 64, 4096
E = H * HD
EPS = 1e-5
FMT = "e4m3"


def layernorm(x, gamma, beta):
    mu = x.mean(-1, keepdims=True)
    var = ((x - mu) ** 2).mean(-1, keepdims=True)
    return (x - mu) * (1.0 / np.sqrt(var + EPS)) * gamma + beta


def heads(y):
    return y.reshape(B, N, H, HD).transpose(0, 2, 1, 3)


def setup_inputs():
    s = mx_kscale(D)
    r = np.random.standard_normal
    x = bf(r((B, N, D)))
    gamma = bf((1.0 + 0.1 * r(D)) * s)
    beta = bf(0.1 * r(D) * s)
    Wq_words, Wq_scales = pack_weight(r((D, E)) * 1.4 / np.sqrt(D) / s[:, None], FMT)
    bq = bf(r(E) * 0.2)
    Wk_words, Wk_scales = pack_weight(r((D, E)) * 1.4 / np.sqrt(D) / s[:, None], FMT)
    bk = bf(r(E) * 0.2)
    Wv_words, Wv_scales = pack_weight(r((D, E)) * 1.0 / np.sqrt(D) / s[:, None], FMT)
    bv = bf(r(E) * 0.2)
    return {"x": x,
            "gamma": gamma, "beta": beta,
            "Wq_words": Wq_words, "Wq_scales": Wq_scales, "bq": bq,
            "Wk_words": Wk_words, "Wk_scales": Wk_scales, "bk": bk,
            "Wv_words": Wv_words, "Wv_scales": Wv_scales, "bv": bv}


def reference(x, gamma, beta, Wq_words, Wq_scales, bq, Wk_words, Wk_scales, bk, Wv_words, Wv_scales, bv):
    h = layernorm(f64(x), f64(gamma), f64(beta))
    hq = mxq(h, 2, "e4m3")
    q = (hq @ unpack_weight(Wq_words, Wq_scales, FMT)) + f64(bq)
    k = (hq @ unpack_weight(Wk_words, Wk_scales, FMT)) + f64(bk)
    v = (hq @ unpack_weight(Wv_words, Wv_scales, FMT)) + f64(bv)
    return heads(q), heads(k), heads(v)

@@ -1,0 +1,252 @@
+from contextlib import ExitStack
+
+import concourse.mybir as mybir
+from concourse.masks import make_identity
+
+F32 = mybir.dt.float32
+BF16 = mybir.dt.bfloat16
+I32 = mybir.dt.int32
+U32 = mybir.dt.uint32
+U8 = mybir.dt.uint8
+FP8X4 = mybir.dt.float8_e4m3fn_x4
+ALU = mybir.AluOpType
+ACT = mybir.ActivationFunctionType
+
+P = 128
+D = 16384
+E = 512
+HEADS = 8
+EPS = 1e-5
+PACK = 4
+K_PASS = P * PACK
+GROUPS = D // K_PASS
+N_W = 3
+
+X_CHUNKS = 4
+X_COLS = D // X_CHUNKS
+STAT_COLS = 512
+G_STEP = 2
+STEPS = GROUPS // G_STEP
+G_LOAD = 4
+ROUNDS = GROUPS // G_LOAD
+W_BUFS = 12
+G_PLANES = 16
+VECTOR_EVERY = 4
+
+FLOPS = 2 * P * D * N_W * E
+
+
+def tile_vit_transformerblock_pa_k_kernel(
+    tc,
+    x,
+    gamma,
+    beta,
+    Wq_words,
+    Wq_scales,
+    bq,
+    Wk_words,
+    Wk_scales,
+    bk,
+    Wv_words,
+    Wv_scales,
+    bv,
+    out_0,
+    out_1,
+    out_2,
+):
+    nc = tc.nc
+    x_rows = x.rearrange("b n d -> (b n) d")
+    words = [w.rearrange("g p n t -> p g (n t)") for w in (Wq_words, Wk_words, Wv_words)]
+    scales = [Wq_scales, Wk_scales, Wv_scales]
+    biases = [bq, bk, bv]
+    outs = [out_0, out_1, out_2]
+
+    with ExitStack() as ctx:
+        keep = ctx.enter_context(tc.tile_pool(name="keep", bufs=1))
+        x_pool = ctx.enter_context(tc.tile_pool(name="x_pool", bufs=X_CHUNKS))
+        w_pool = ctx.enter_context(tc.tile_pool(name="w_pool", bufs=W_BUFS))
+        work = ctx.enter_context(tc.tile_pool(name="work", bufs=3))
+        h_pool = ctx.enter_context(tc.tile_pool(name="h_pool", bufs=STEPS))
+        acc_pool = ctx.enter_context(tc.psum_pool(name="acc_pool", bufs=1))
+        t_pool = ctx.enter_context(tc.psum_pool(name="t_pool", bufs=4))
+
+        x_tiles = []
+        for c in range(X_CHUNKS):
+            x_chunk = x_pool.tile([P, X_COLS], BF16, name="x_chunk", tag="x_chunk")
+            nc.sync.dma_start(out=x_chunk[:], in_=x_rows[:, c * X_COLS : (c + 1) * X_COLS])
+            x_tiles.append(x_chunk)
+
+        gb_rows = keep.tile([P, K_PASS], BF16)
+        nc.vector.memset(gb_rows[:], 0.0)
+        nc.scalar.dma_start(out=gb_rows[0:GROUPS, :], in_=gamma.rearrange("(g c) -> g c", c=K_PASS))
+        nc.scalar.dma_start(
+            out=gb_rows[GROUPS : 2 * GROUPS, :], in_=beta.rearrange("(g c) -> g c", c=K_PASS)
+        )
+        bias_rows = keep.tile([P, N_W, E], BF16)
+        nc.vector.memset(bias_rows[:], 0.0)
+        for w in range(N_W):
+            nc.scalar.dma_start(
+                out=bias_rows[0:1, w, :], in_=biases[w].rearrange("(o e) -> o e", o=1)
+            )
+
+        plane_tiles = []
+        for half in range(GROUPS // G_PLANES):
+            planes = keep.tile(
+                [P, G_PLANES, E], U8, name="planes%d" % half, align_bytes=64
+            )
+            nc.vector.memset(planes[:].rearrange("p g n -> p (g n)").bitcast(I32), 0)
+            plane_tiles.append(planes)
+        ident = keep.tile([P, P], F32)
+        make_identity(nc, ident[:])
+        for half in range(GROUPS // G_PLANES):
+            g_range = slice(half * G_PLANES, (half + 1) * G_PLANES)
+            for w in range(N_W):
+                for quad in range(4):
+                    first = 32 * quad + PACK * w
+                    nc.gpsimd.dma_start(
+                        out=plane_tiles[half][first : first + 4, :, :].bitcast(F32),
+                        in_=scales[w][g_range, 4 * quad : 4 * quad + 4, :]
+                        .rearrange("g r n -> r g n")
+                        .bitcast(F32),
+                    )
+
+        loads = [(r, w) for r in range(ROUNDS) for w in range(N_W)]
+        w_tiles = {}
+
+        def load_weights(i):
+            r, w = loads[i]
+            w_chunk = w_pool.tile([P, G_LOAD, E], U32, name="w_chunk", tag="w_chunk", align_bytes=64)
+            nc.sync.dma_start(
+                out=w_chunk[:].bitcast(I32),
+                in_=words[w][:, r * G_LOAD : (r + 1) * G_LOAD, :].bitcast(I32),
+            )
+            w_tiles[(r, w)] = w_chunk
+
+        for i in range(W_BUFS):
+            load_weights(i)
+
+        warm = keep.tile([P, 1], F32)
+        nc.vector.memset(warm[:], 1.0)
+        nc.scalar.activation(out=warm[:], in_=warm[:], func=ACT.Sqrt)
+
+        gb_sorted = keep.tile([P, PACK, P], F32)
+        nc.vector.tensor_copy(
+            out=gb_sorted[:].rearrange("r t p -> r p t"),
+            in_=gb_rows[:].rearrange("r (p t) -> r p t", t=PACK),
+        )
+        gb_bank = t_pool.tile([P, PACK, P], F32, name="gb_bank", tag="bank")
+        for t in range(PACK):
+            nc.tensor.transpose(out=gb_bank[:, t, :], in_=gb_sorted[:, t, :], identity=ident[:])
+        gb = keep.tile([P, PACK, P], F32)
+        nc.vector.tensor_copy(out=gb[:], in_=gb_bank[:])
+
+        ones = keep.tile([P, P], BF16)
+        nc.vector.memset(ones[:], 1.0)
+        bias_all = keep.tile([P, N_W, E], F32)
+        for w in range(N_W):
+            bias_bank = t_pool.tile([P, E], F32, name="bias_bank", tag="bank")
+            nc.tensor.matmul(
+                out=bias_bank[:], lhsT=ones[:], rhs=bias_rows[:, w, :], start=True, stop=True
+            )
+            nc.scalar.copy(out=bias_all[:, w, :], in_=bias_bank[:])
+
+        n_stats = D // STAT_COLS
+        stats = keep.tile([P, n_stats, 6], F32)
+        for i in range(n_stats):
+            c, j = divmod(i, X_COLS // STAT_COLS)
+            nc.vector.bn_stats(
+                out=stats[:, i, :], in_=x_tiles[c][:, j * STAT_COLS : (j + 1) * STAT_COLS]
+            )
+        mean_var = keep.tile([P, 2], F32)
+        nc.vector.bn_aggr(out=mean_var[:], in_=stats[:].rearrange("p c s -> p (c s)"))
+        var_eps = keep.tile([P, 1], F32)
+        nc.vector.tensor_scalar(
+            out=var_eps[:], in0=mean_var[:, 1:2], scalar1=EPS, scalar2=None, op0=ALU.add
+        )
+        std = keep.tile([P, 1], F32)
+        nc.scalar.activation(out=std[:], in_=var_eps[:], func=ACT.Sqrt)
+        rstd = keep.tile([P, 1], F32)
+        nc.vector.reciprocal(out=rstd[:], in_=std[:])
+
+        h_codes = []
+        h_scales = []
+
+        def make_h(s):
+            c, j = divmod(s, X_COLS // (G_STEP * K_PASS))
+            x_part = x_tiles[c][:, j * G_STEP * K_PASS : (j + 1) * G_STEP * K_PASS]
+            xn = work.tile([P, G_STEP, PACK, P], F32, name="xn", tag="xn")
+            nc.vector.tensor_scalar(
+                out=xn[:].rearrange("r g t p -> r g p t"),
+                in0=x_part.rearrange("r (g p t) -> r g p t", g=G_STEP, t=PACK),
+                scalar1=mean_var[:, 0:1],
+                scalar2=rstd[:, 0:1],
+                op0=ALU.subtract,
+                op1=ALU.mult,
+            )
+            h_planes = work.tile([P, G_STEP, PACK, P], BF16, name="h_planes", tag="h_planes")
+            for gi in range(G_STEP):
+                g = s * G_STEP + gi
+                bank = t_pool.tile([P, PACK, P], F32, name="bank", tag="bank")
+                for t in range(PACK):
+                    nc.tensor.transpose(out=bank[:, t, :], in_=xn[:, gi, t, :], identity=ident[:])
+                for t in range(PACK):
+                    if g % VECTOR_EVERY == 0:
+                        nc.vector.tensor_scalar(
+                            out=h_planes[:, gi, t, :],
+                            in0=bank[:, t, :],
+                            scalar1=gb[:, t, g : g + 1],
+                            scalar2=gb[:, t, GROUPS + g : GROUPS + g + 1],
+                            op0=ALU.mult,
+                            op1=ALU.add,
+                        )
+                    else:
+                        nc.scalar.activation(
+                            out=h_planes[:, gi, t, :],
+                            in_=bank[:, t, :],
+                            func=ACT.Identity,
+                            scale=gb[:, t, g : g + 1],
+                            bias=gb[:, t, GROUPS + g : GROUPS + g + 1],
+                        )
+            grouped = work.tile([P, G_STEP, P, PACK], BF16, name="grouped", tag="grouped", align_bytes=64)
+            nc.vector.tensor_copy(out=grouped[:], in_=h_planes[:].rearrange("p g t r -> p g r t"))
+            codes = h_pool.tile([P, G_STEP * P], U32, name="codes", tag="codes", align_bytes=64)
+            code_scales = h_pool.tile(
+                [P, G_STEP * P], U8, name="code_scales", tag="code_scales", align_bytes=64
+            )
+            nc.vector.quantize_mx(
+                out=codes[:].bitcast(FP8X4),
+                scales=code_scales[:],
+                in_=grouped[:].rearrange("p g r t -> p (g r t)"),
+            )
+            h_codes.append(codes)
+            h_scales.append(code_scales)
+
+        acc = [acc_pool.tile([P, E], F32, name="acc%d" % w) for w in range(N_W)]
+        for r in range(ROUNDS):
+            for s in range(r * G_LOAD // G_STEP, (r + 1) * G_LOAD // G_STEP):
+                make_h(s)
+            for w in range(N_W):
+                for gl in range(G_LOAD):
+                    g = r * G_LOAD + gl
+                    s, gi = divmod(g, G_STEP)
+                    half, gp = divmod(g, G_PLANES)
+                    nc.tensor.matmul_mx(
+                        out=acc[w][:],
+                        lhsT=h_codes[s][:, gi * P : (gi + 1) * P].bitcast(FP8X4),
+                        lhsT_scale=h_scales[s][:, gi * P : (gi + 1) * P],
+                        rhs=w_tiles[(r, w)][:, gl, :].bitcast(FP8X4),
+                        rhs_scale=plane_tiles[half][PACK * w : P, gp, :],
+                        start=(g == 0),
+                        stop=(g == GROUPS - 1),
+                    )
+                if r * N_W + w + W_BUFS < len(loads):
+                    load_weights(r * N_W + w + W_BUFS)
+
+        for w in range(N_W):
+            result = work.tile([P, E], F32, name="result", tag="result")
+            nc.vector.tensor_tensor(out=result[:], in0=acc[w][:], in1=bias_all[:, w, :], op=ALU.add)
+            for b in range(2):
+                nc.sync.dma_start(
+                    out=outs[w][b].rearrange("a n d -> n a d"),
+                    in_=result[b * 64 : (b + 1) * 64, :].rearrange("n (a d) -> n a d", a=HEADS),
+                )

@@ -131,8 +131,7 @@ def tile_vit_transformerblock_pa_k_kernel(
 
         gb_sorted = keep.tile([P, PACK, P], F32)
         nc.vector.tensor_copy(
-            out=gb_sorted[:].rearrange("r t p -> r p t"),
-            in_=gb_rows[:].rearrange("r (p t) -> r p t", t=PACK),
+            out=gb_sorted[:], in_=gb_rows[:].rearrange("r (p t) -> r t p", t=PACK)
         )
         gb_bank = t_pool.tile([P, PACK, P], F32, name="gb_bank", tag="bank")
         for t in range(PACK):
@@ -176,8 +175,8 @@ def tile_vit_transformerblock_pa_k_kernel(
             x_part = x_tiles[c][:, j * G_STEP * K_PASS : (j + 1) * G_STEP * K_PASS]
             xn = work.tile([P, G_STEP, PACK, P], F32, name="xn", tag="xn")
             nc.vector.tensor_scalar(
-                out=xn[:].rearrange("r g t p -> r g p t"),
-                in0=x_part.rearrange("r (g p t) -> r g p t", g=G_STEP, t=PACK),
+                out=xn[:],
+                in0=x_part.rearrange("r (g p t) -> r g t p", g=G_STEP, t=PACK),
                 scalar1=mean_var[:, 0:1],
                 scalar2=rstd[:, 0:1],
                 op0=ALU.subtract,

@@ -25,13 +25,12 @@ N_W = 3
 X_CHUNKS = 4
 X_COLS = D // X_CHUNKS
 STAT_COLS = 512
-G_STEP = 2
-STEPS = GROUPS // G_STEP
-G_LOAD = 4
-ROUNDS = GROUPS // G_LOAD
+VECTOR_BLOCKS = 6
+SCALAR_COLS = X_COLS - VECTOR_BLOCKS * STAT_COLS
+G_ROUND = 4
+ROUNDS = GROUPS // G_ROUND
 W_BUFS = 12
-G_PLANES = 16
-VECTOR_EVERY = 4
+T_BANKS = 5
 
 FLOPS = 2 * P * D * N_W * E
 
@@ -65,10 +64,12 @@ def tile_vit_transformerblock_pa_k_kernel(
         keep = ctx.enter_context(tc.tile_pool(name="keep", bufs=1))
         x_pool = ctx.enter_context(tc.tile_pool(name="x_pool", bufs=X_CHUNKS))
         w_pool = ctx.enter_context(tc.tile_pool(name="w_pool", bufs=W_BUFS))
-        work = ctx.enter_context(tc.tile_pool(name="work", bufs=3))
-        h_pool = ctx.enter_context(tc.tile_pool(name="h_pool", bufs=STEPS))
+        work = ctx.enter_context(tc.tile_pool(name="work", bufs=2))
+        h_pool = ctx.enter_context(tc.tile_pool(name="h_pool", bufs=ROUNDS))
+        out_pool = ctx.enter_context(tc.tile_pool(name="out_pool", bufs=N_W))
         acc_pool = ctx.enter_context(tc.psum_pool(name="acc_pool", bufs=1))
-        t_pool = ctx.enter_context(tc.psum_pool(name="t_pool", bufs=4))
+        t_pool = ctx.enter_context(tc.psum_pool(name="t_pool", bufs=T_BANKS))
+        ctx.enter_context(tc.manual_schedule())
 
         x_tiles = []
         for c in range(X_CHUNKS):
@@ -89,58 +90,49 @@ def tile_vit_transformerblock_pa_k_kernel(
                 out=bias_rows[0:1, w, :], in_=biases[w].rearrange("(o e) -> o e", o=1)
             )
 
-        plane_tiles = []
-        for half in range(GROUPS // G_PLANES):
-            planes = keep.tile(
-                [P, G_PLANES, E], U8, name="planes%d" % half, align_bytes=64
-            )
-            nc.vector.memset(planes[:].rearrange("p g n -> p (g n)").bitcast(I32), 0)
-            plane_tiles.append(planes)
+        planes = keep.tile([P, GROUPS, E], U8, align_bytes=64)
+        nc.vector.memset(planes[:].rearrange("p g n -> p (g n)").bitcast(I32), 0)
         ident = keep.tile([P, P], F32)
         make_identity(nc, ident[:])
-        for half in range(GROUPS // G_PLANES):
-            g_range = slice(half * G_PLANES, (half + 1) * G_PLANES)
-            for w in range(N_W):
-                for quad in range(4):
-                    first = 32 * quad + PACK * w
-                    nc.gpsimd.dma_start(
-                        out=plane_tiles[half][first : first + 4, :, :].bitcast(F32),
-                        in_=scales[w][g_range, 4 * quad : 4 * quad + 4, :]
-                        .rearrange("g r n -> r g n")
-                        .bitcast(F32),
-                    )
+        for w in range(N_W):
+            for quad in range(4):
+                first = 32 * quad + PACK * w
+                nc.gpsimd.dma_start(
+                    out=planes[first : first + 4, :, :].bitcast(F32),
+                    in_=scales[w][:, 4 * quad : 4 * quad + 4, :]
+                    .rearrange("g r n -> r g n")
+                    .bitcast(F32),
+                )
 
         loads = [(r, w) for r in range(ROUNDS) for w in range(N_W)]
         w_tiles = {}
 
         def load_weights(i):
             r, w = loads[i]
-            w_chunk = w_pool.tile([P, G_LOAD, E], U32, name="w_chunk", tag="w_chunk", align_bytes=64)
+            w_chunk = w_pool.tile([P, G_ROUND, E], U32, name="w_chunk", tag="w_chunk", align_bytes=64)
             nc.sync.dma_start(
                 out=w_chunk[:].bitcast(I32),
-                in_=words[w][:, r * G_LOAD : (r + 1) * G_LOAD, :].bitcast(I32),
+                in_=words[w][:, r * G_ROUND : (r + 1) * G_ROUND, :].bitcast(I32),
             )
             w_tiles[(r, w)] = w_chunk
 
         for i in range(W_BUFS):
             load_weights(i)
 
+        ones = keep.tile([P, P], BF16)
+        nc.vector.memset(ones[:], 1.0)
         warm = keep.tile([P, 1], F32)
         nc.vector.memset(warm[:], 1.0)
         nc.scalar.activation(out=warm[:], in_=warm[:], func=ACT.Sqrt)
 
         gb_sorted = keep.tile([P, PACK, P], F32)
-        nc.vector.tensor_copy(
-            out=gb_sorted[:], in_=gb_rows[:].rearrange("r (p t) -> r t p", t=PACK)
-        )
+        nc.scalar.copy(out=gb_sorted[:], in_=gb_rows[:].rearrange("r (p t) -> r t p", t=PACK))
         gb_bank = t_pool.tile([P, PACK, P], F32, name="gb_bank", tag="bank")
         for t in range(PACK):
             nc.tensor.transpose(out=gb_bank[:, t, :], in_=gb_sorted[:, t, :], identity=ident[:])
         gb = keep.tile([P, PACK, P], F32)
-        nc.vector.tensor_copy(out=gb[:], in_=gb_bank[:])
+        nc.scalar.copy(out=gb[:], in_=gb_bank[:])
 
-        ones = keep.tile([P, P], BF16)
-        nc.vector.memset(ones[:], 1.0)
         bias_all = keep.tile([P, N_W, E], F32)
         for w in range(N_W):
             bias_bank = t_pool.tile([P, E], F32, name="bias_bank", tag="bank")
@@ -149,15 +141,37 @@ def tile_vit_transformerblock_pa_k_kernel(
             )
             nc.scalar.copy(out=bias_all[:, w, :], in_=bias_bank[:])
 
-        n_stats = D // STAT_COLS
-        stats = keep.tile([P, n_stats, 6], F32)
-        for i in range(n_stats):
-            c, j = divmod(i, X_COLS // STAT_COLS)
-            nc.vector.bn_stats(
-                out=stats[:, i, :], in_=x_tiles[c][:, j * STAT_COLS : (j + 1) * STAT_COLS]
+        vector_stats = X_CHUNKS * VECTOR_BLOCKS * 6
+        stats = keep.tile([P, vector_stats + X_CHUNKS * 3], F32)
+        nc.vector.memset(stats[:, vector_stats:], float(SCALAR_COLS))
+        part_sum = keep.tile([P, X_CHUNKS], F32)
+        neg_mean = keep.tile([P, X_CHUNKS], F32)
+        unused = keep.tile([P, SCALAR_COLS], BF16)
+        for c in range(X_CHUNKS):
+            for j in range(VECTOR_BLOCKS):
+                i = c * VECTOR_BLOCKS + j
+                nc.vector.bn_stats(
+                    out=stats[:, 6 * i : 6 * i + 6],
+                    in_=x_tiles[c][:, j * STAT_COLS : (j + 1) * STAT_COLS],
+                )
+            part = x_tiles[c][:, VECTOR_BLOCKS * STAT_COLS :]
+            triple = vector_stats + 3 * c
+            nc.scalar.activation(
+                out=unused[:], in_=part, func=ACT.Copy, accum_out=part_sum[:, c : c + 1]
+            )
+            nc.scalar.mul(
+                out=stats[:, triple + 1 : triple + 2], in_=part_sum[:, c : c + 1], mul=1.0 / SCALAR_COLS
+            )
+            nc.scalar.mul(out=neg_mean[:, c : c + 1], in_=part_sum[:, c : c + 1], mul=-1.0 / SCALAR_COLS)
+            nc.scalar.activation(
+                out=unused[:],
+                in_=part,
+                func=ACT.Square,
+                bias=neg_mean[:, c : c + 1],
+                accum_out=stats[:, triple + 2 : triple + 3],
             )
         mean_var = keep.tile([P, 2], F32)
-        nc.vector.bn_aggr(out=mean_var[:], in_=stats[:].rearrange("p c s -> p (c s)"))
+        nc.vector.bn_aggr(out=mean_var[:], in_=stats[:])
         var_eps = keep.tile([P, 1], F32)
         nc.vector.tensor_scalar(
             out=var_eps[:], in0=mean_var[:, 1:2], scalar1=EPS, scalar2=None, op0=ALU.add
@@ -167,85 +181,105 @@ def tile_vit_transformerblock_pa_k_kernel(
         rstd = keep.tile([P, 1], F32)
         nc.vector.reciprocal(out=rstd[:], in_=std[:])
 
-        h_codes = []
-        h_scales = []
+        xn_tiles = {}
+        bank_tiles = {}
+        plane_tiles = {}
+        h_codes = {}
+        h_scales = {}
+        acc = [acc_pool.tile([P, E], F32, name="acc%d" % w) for w in range(N_W)]
 
-        def make_h(s):
-            c, j = divmod(s, X_COLS // (G_STEP * K_PASS))
-            x_part = x_tiles[c][:, j * G_STEP * K_PASS : (j + 1) * G_STEP * K_PASS]
-            xn = work.tile([P, G_STEP, PACK, P], F32, name="xn", tag="xn")
+        def normalise(r):
+            c, j = divmod(r, X_COLS // (G_ROUND * K_PASS))
+            x_part = x_tiles[c][:, j * G_ROUND * K_PASS : (j + 1) * G_ROUND * K_PASS]
+            xn = work.tile([P, G_ROUND, PACK, P], F32, name="xn", tag="xn")
             nc.vector.tensor_scalar(
                 out=xn[:],
-                in0=x_part.rearrange("r (g p t) -> r g t p", g=G_STEP, t=PACK),
+                in0=x_part.rearrange("r (g p t) -> r g t p", g=G_ROUND, t=PACK),
                 scalar1=mean_var[:, 0:1],
                 scalar2=rstd[:, 0:1],
                 op0=ALU.subtract,
                 op1=ALU.mult,
             )
-            h_planes = work.tile([P, G_STEP, PACK, P], BF16, name="h_planes", tag="h_planes")
-            for gi in range(G_STEP):
-                g = s * G_STEP + gi
+            xn_tiles[r] = xn
+
+        def transpose(r):
+            bank_tiles[r] = []
+            for gi in range(G_ROUND):
                 bank = t_pool.tile([P, PACK, P], F32, name="bank", tag="bank")
                 for t in range(PACK):
-                    nc.tensor.transpose(out=bank[:, t, :], in_=xn[:, gi, t, :], identity=ident[:])
+                    nc.tensor.transpose(
+                        out=bank[:, t, :], in_=xn_tiles[r][:, gi, t, :], identity=ident[:]
+                    )
+                bank_tiles[r].append(bank)
+
+        def scale_and_shift(r):
+            h_planes = work.tile([P, G_ROUND, PACK, P], BF16, name="h_planes", tag="h_planes")
+            for gi in range(G_ROUND):
+                g = r * G_ROUND + gi
                 for t in range(PACK):
-                    if g % VECTOR_EVERY == 0:
-                        nc.vector.tensor_scalar(
-                            out=h_planes[:, gi, t, :],
-                            in0=bank[:, t, :],
-                            scalar1=gb[:, t, g : g + 1],
-                            scalar2=gb[:, t, GROUPS + g : GROUPS + g + 1],
-                            op0=ALU.mult,
-                            op1=ALU.add,
-                        )
-                    else:
-                        nc.scalar.activation(
-                            out=h_planes[:, gi, t, :],
-                            in_=bank[:, t, :],
-                            func=ACT.Identity,
-                            scale=gb[:, t, g : g + 1],
-                            bias=gb[:, t, GROUPS + g : GROUPS + g + 1],
-                        )
-            grouped = work.tile([P, G_STEP, P, PACK], BF16, name="grouped", tag="grouped", align_bytes=64)
-            nc.vector.tensor_copy(out=grouped[:], in_=h_planes[:].rearrange("p g t r -> p g r t"))
-            codes = h_pool.tile([P, G_STEP * P], U32, name="codes", tag="codes", align_bytes=64)
+                    nc.scalar.activation(
+                        out=h_planes[:, gi, t, :],
+                        in_=bank_tiles[r][gi][:, t, :],
+                        func=ACT.Identity,
+                        scale=gb[:, t, g : g + 1],
+                        bias=gb[:, t, GROUPS + g : GROUPS + g + 1],
+                    )
+            plane_tiles[r] = h_planes
+
+        def quantise(r):
+            grouped = work.tile([P, G_ROUND, P, PACK], BF16, name="grouped", tag="grouped", align_bytes=64)
+            nc.vector.tensor_copy(
+                out=grouped[:], in_=plane_tiles[r][:].rearrange("p g t r -> p g r t")
+            )
+            codes = h_pool.tile([P, G_ROUND * P], U32, name="codes", tag="codes", align_bytes=64)
             code_scales = h_pool.tile(
-                [P, G_STEP * P], U8, name="code_scales", tag="code_scales", align_bytes=64
+                [P, G_ROUND * P], U8, name="code_scales", tag="code_scales", align_bytes=64
             )
             nc.vector.quantize_mx(
                 out=codes[:].bitcast(FP8X4),
                 scales=code_scales[:],
                 in_=grouped[:].rearrange("p g r t -> p (g r t)"),
             )
-            h_codes.append(codes)
-            h_scales.append(code_scales)
+            h_codes[r] = codes
+            h_scales[r] = code_scales
 
-        acc = [acc_pool.tile([P, E], F32, name="acc%d" % w) for w in range(N_W)]
-        for r in range(ROUNDS):
-            for s in range(r * G_LOAD // G_STEP, (r + 1) * G_LOAD // G_STEP):
-                make_h(s)
+        def multiply(r):
             for w in range(N_W):
-                for gl in range(G_LOAD):
-                    g = r * G_LOAD + gl
-                    s, gi = divmod(g, G_STEP)
-                    half, gp = divmod(g, G_PLANES)
+                for gi in range(G_ROUND):
+                    g = r * G_ROUND + gi
                     nc.tensor.matmul_mx(
                         out=acc[w][:],
-                        lhsT=h_codes[s][:, gi * P : (gi + 1) * P].bitcast(FP8X4),
-                        lhsT_scale=h_scales[s][:, gi * P : (gi + 1) * P],
-                        rhs=w_tiles[(r, w)][:, gl, :].bitcast(FP8X4),
-                        rhs_scale=plane_tiles[half][PACK * w : P, gp, :],
+                        lhsT=h_codes[r][:, gi * P : (gi + 1) * P].bitcast(FP8X4),
+                        lhsT_scale=h_scales[r][:, gi * P : (gi + 1) * P],
+                        rhs=w_tiles[(r, w)][:, gi, :].bitcast(FP8X4),
+                        rhs_scale=planes[PACK * w : P, g, :],
                         start=(g == 0),
                         stop=(g == GROUPS - 1),
                     )
                 if r * N_W + w + W_BUFS < len(loads):
                     load_weights(r * N_W + w + W_BUFS)
+                if r == ROUNDS - 1:
+                    finish(w)
 
-        for w in range(N_W):
-            result = work.tile([P, E], F32, name="result", tag="result")
+        def finish(w):
+            result = out_pool.tile([P, E], F32, name="result", tag="result")
             nc.vector.tensor_tensor(out=result[:], in0=acc[w][:], in1=bias_all[:, w, :], op=ALU.add)
             for b in range(2):
                 nc.sync.dma_start(
                     out=outs[w][b].rearrange("a n d -> n a d"),
                     in_=result[b * 64 : (b + 1) * 64, :].rearrange("n (a d) -> n a d", a=HEADS),
                 )
+
+        normalise(0)
+        transpose(0)
+        normalise(1)
+        for r in range(ROUNDS):
+            scale_and_shift(r)
+            if r + 1 < ROUNDS:
+                transpose(r + 1)
+            if r + 2 < ROUNDS:
+                normalise(r + 2)
+            quantise(r)
+            if r >= 1:
+                multiply(r - 1)
+        multiply(ROUNDS - 1)

@@ -92,17 +92,14 @@ def tile_vit_transformerblock_pa_k_kernel(
 
         planes = keep.tile([P, GROUPS, E], U8, align_bytes=64)
         nc.vector.memset(planes[:].rearrange("p g n -> p (g n)").bitcast(I32), 0)
+        for r in range(4):
+            for w in range(N_W):
+                nc.sync.dma_start(
+                    out=planes[PACK * w + r : P : 32, :, :].bitcast(I32),
+                    in_=scales[w][:, r : 16 : 4, :].rearrange("g q n -> q g n").bitcast(I32),
+                )
         ident = keep.tile([P, P], F32)
         make_identity(nc, ident[:])
-        for w in range(N_W):
-            for quad in range(4):
-                first = 32 * quad + PACK * w
-                nc.gpsimd.dma_start(
-                    out=planes[first : first + 4, :, :].bitcast(F32),
-                    in_=scales[w][:, 4 * quad : 4 * quad + 4, :]
-                    .rearrange("g r n -> r g n")
-                    .bitcast(F32),
-                )
 
         loads = [(r, w) for r in range(ROUNDS) for w in range(N_W)]
         w_tiles = {}

@@ -31,6 +31,7 @@ G_ROUND = 4
 ROUNDS = GROUPS // G_ROUND
 W_BUFS = 12
 T_BANKS = 5
+G_PLANES = GROUPS // 2
 
 FLOPS = 2 * P * D * N_W * E
 
@@ -90,16 +91,25 @@ def tile_vit_transformerblock_pa_k_kernel(
                 out=bias_rows[0:1, w, :], in_=biases[w].rearrange("(o e) -> o e", o=1)
             )
 
-        planes = keep.tile([P, GROUPS, E], U8, align_bytes=64)
-        nc.vector.memset(planes[:].rearrange("p g n -> p (g n)").bitcast(I32), 0)
+        ident = keep.tile([P, P], F32)
+        make_identity(nc, ident[:])
+        planes = []
+        for half in range(GROUPS // G_PLANES):
+            plane_tile = keep.tile([P, G_PLANES, E], U8, name="planes%d" % half, align_bytes=64)
+            nc.vector.memset(plane_tile[:].rearrange("p g n -> p (g n)").bitcast(I32), 0)
+            planes.append(plane_tile)
         for r in range(4):
             for w in range(N_W):
                 nc.sync.dma_start(
-                    out=planes[PACK * w + r : P : 32, :, :].bitcast(I32),
-                    in_=scales[w][:, r : 16 : 4, :].rearrange("g q n -> q g n").bitcast(I32),
+                    out=planes[0][PACK * w + r : P : 32, :, :].bitcast(I32),
+                    in_=scales[w][0:G_PLANES, r : 16 : 4, :].rearrange("g q n -> q g n").bitcast(I32),
                 )
-        ident = keep.tile([P, P], F32)
-        make_identity(nc, ident[:])
+                nc.gpsimd.dma_start(
+                    out=planes[1][PACK * w + r : P : 32, :, :].bitcast(F32),
+                    in_=scales[w][G_PLANES:GROUPS, r : 16 : 4, :]
+                    .rearrange("g q n -> q g n")
+                    .bitcast(F32),
+                )
 
         loads = [(r, w) for r in range(ROUNDS) for w in range(N_W)]
         w_tiles = {}
@@ -249,7 +259,7 @@ def tile_vit_transformerblock_pa_k_kernel(
                         lhsT=h_codes[r][:, gi * P : (gi + 1) * P].bitcast(FP8X4),
                         lhsT_scale=h_scales[r][:, gi * P : (gi + 1) * P],
                         rhs=w_tiles[(r, w)][:, gi, :].bitcast(FP8X4),
-                        rhs_scale=planes[PACK * w : P, g, :],
+                        rhs_scale=planes[g // G_PLANES][PACK * w : P, g % G_PLANES, :],
                         start=(g == 0),
                         stop=(g == GROUPS - 1),
                     )

@@ -13,6 +13,8 @@ ALU = mybir.AluOpType
 ACT = mybir.ActivationFunctionType
 
 P = 128
+BATCH = 2
+TOKENS = 64
 D = 16384
 E = 512
 HEADS = 8
@@ -21,17 +23,22 @@ PACK = 4
 K_PASS = P * PACK
 GROUPS = D // K_PASS
 N_W = 3
+SCALE_ROWS = K_PASS // 32
+QUADRANT = 32
 
 X_CHUNKS = 4
 X_COLS = D // X_CHUNKS
 STAT_COLS = 512
+STATS_OUT = 6
+TRIPLE = 3
 VECTOR_BLOCKS = 6
 SCALAR_COLS = X_COLS - VECTOR_BLOCKS * STAT_COLS
 G_ROUND = 4
 ROUNDS = GROUPS // G_ROUND
 W_BUFS = 12
 T_BANKS = 5
-G_PLANES = GROUPS // 2
+SCALE_BATCH = 2 * N_W
+SCALE_BATCHES = N_W * SCALE_ROWS // SCALE_BATCH
 
 FLOPS = 2 * P * D * N_W * E
 
@@ -56,7 +63,9 @@ def tile_vit_transformerblock_pa_k_kernel(
 ):
     nc = tc.nc
     x_rows = x.rearrange("b n d -> (b n) d")
-    words = [w.rearrange("g p n t -> p g (n t)") for w in (Wq_words, Wk_words, Wv_words)]
+    words = [
+        packed.rearrange("g p n t -> p g (n t)") for packed in (Wq_words, Wk_words, Wv_words)
+    ]
     scales = [Wq_scales, Wk_scales, Wv_scales]
     biases = [bq, bk, bv]
     outs = [out_0, out_1, out_2]
@@ -72,44 +81,26 @@ def tile_vit_transformerblock_pa_k_kernel(
         t_pool = ctx.enter_context(tc.psum_pool(name="t_pool", bufs=T_BANKS))
         ctx.enter_context(tc.manual_schedule())
 
+        planes = keep.tile([P, GROUPS, E], U8, align_bytes=64)
+        nc.vector.memset(planes[:].rearrange("p g n -> p (g n)").bitcast(I32), 0)
+
+        def load_scales(i):
+            s, low = divmod(i, 2)
+            for high in range(2):
+                for w in range(N_W):
+                    q = PACK * (2 * high + low) + s
+                    row = QUADRANT * (2 * high + low) + PACK * w + s
+                    nc.sync.dma_start(
+                        out=planes[row : row + 1, :, :].bitcast(I32),
+                        in_=scales[w][:, q : q + 1, :].rearrange("g o n -> o g n").bitcast(I32),
+                    )
+
         x_tiles = []
-        for c in range(X_CHUNKS):
+
+        def load_x(c):
             x_chunk = x_pool.tile([P, X_COLS], BF16, name="x_chunk", tag="x_chunk")
             nc.sync.dma_start(out=x_chunk[:], in_=x_rows[:, c * X_COLS : (c + 1) * X_COLS])
             x_tiles.append(x_chunk)
-
-        gb_rows = keep.tile([P, K_PASS], BF16)
-        nc.vector.memset(gb_rows[:], 0.0)
-        nc.scalar.dma_start(out=gb_rows[0:GROUPS, :], in_=gamma.rearrange("(g c) -> g c", c=K_PASS))
-        nc.scalar.dma_start(
-            out=gb_rows[GROUPS : 2 * GROUPS, :], in_=beta.rearrange("(g c) -> g c", c=K_PASS)
-        )
-        bias_rows = keep.tile([P, N_W, E], BF16)
-        nc.vector.memset(bias_rows[:], 0.0)
-        for w in range(N_W):
-            nc.scalar.dma_start(
-                out=bias_rows[0:1, w, :], in_=biases[w].rearrange("(o e) -> o e", o=1)
-            )
-
-        ident = keep.tile([P, P], F32)
-        make_identity(nc, ident[:])
-        planes = []
-        for half in range(GROUPS // G_PLANES):
-            plane_tile = keep.tile([P, G_PLANES, E], U8, name="planes%d" % half, align_bytes=64)
-            nc.vector.memset(plane_tile[:].rearrange("p g n -> p (g n)").bitcast(I32), 0)
-            planes.append(plane_tile)
-        for r in range(4):
-            for w in range(N_W):
-                nc.sync.dma_start(
-                    out=planes[0][PACK * w + r : P : 32, :, :].bitcast(I32),
-                    in_=scales[w][0:G_PLANES, r : 16 : 4, :].rearrange("g q n -> q g n").bitcast(I32),
-                )
-                nc.gpsimd.dma_start(
-                    out=planes[1][PACK * w + r : P : 32, :, :].bitcast(F32),
-                    in_=scales[w][G_PLANES:GROUPS, r : 16 : 4, :]
-                    .rearrange("g q n -> q g n")
-                    .bitcast(F32),
-                )
 
         loads = [(r, w) for r in range(ROUNDS) for w in range(N_W)]
         w_tiles = {}
@@ -123,9 +114,29 @@ def tile_vit_transformerblock_pa_k_kernel(
             )
             w_tiles[(r, w)] = w_chunk
 
-        for i in range(W_BUFS):
-            load_weights(i)
+        for i in range(X_CHUNKS + W_BUFS):
+            if i < X_CHUNKS:
+                load_x(i)
+            else:
+                load_weights(i - X_CHUNKS)
+            if 1 <= i <= SCALE_BATCHES:
+                load_scales(i - 1)
 
+        gb_rows = keep.tile([P, K_PASS], BF16)
+        nc.vector.memset(gb_rows[:], 0.0)
+        nc.scalar.dma_start(out=gb_rows[0:GROUPS, :], in_=gamma.rearrange("(g k) -> g k", k=K_PASS))
+        nc.scalar.dma_start(
+            out=gb_rows[GROUPS : 2 * GROUPS, :], in_=beta.rearrange("(g k) -> g k", k=K_PASS)
+        )
+        bias_rows = keep.tile([P, N_W, E], BF16)
+        nc.vector.memset(bias_rows[:], 0.0)
+        for w in range(N_W):
+            nc.scalar.dma_start(
+                out=bias_rows[0:1, w, :], in_=biases[w].rearrange("(o e) -> o e", o=1)
+            )
+
+        ident = keep.tile([P, P], F32)
+        make_identity(nc, ident[:])
         ones = keep.tile([P, P], BF16)
         nc.vector.memset(ones[:], 1.0)
         warm = keep.tile([P, 1], F32)
@@ -133,7 +144,7 @@ def tile_vit_transformerblock_pa_k_kernel(
         nc.scalar.activation(out=warm[:], in_=warm[:], func=ACT.Sqrt)
 
         gb_sorted = keep.tile([P, PACK, P], F32)
-        nc.scalar.copy(out=gb_sorted[:], in_=gb_rows[:].rearrange("r (p t) -> r t p", t=PACK))
+        nc.scalar.copy(out=gb_sorted[:], in_=gb_rows[:].rearrange("m (p t) -> m t p", t=PACK))
         gb_bank = t_pool.tile([P, PACK, P], F32, name="gb_bank", tag="bank")
         for t in range(PACK):
             nc.tensor.transpose(out=gb_bank[:, t, :], in_=gb_sorted[:, t, :], identity=ident[:])
@@ -148,8 +159,8 @@ def tile_vit_transformerblock_pa_k_kernel(
             )
             nc.scalar.copy(out=bias_all[:, w, :], in_=bias_bank[:])
 
-        vector_stats = X_CHUNKS * VECTOR_BLOCKS * 6
-        stats = keep.tile([P, vector_stats + X_CHUNKS * 3], F32)
+        vector_stats = X_CHUNKS * VECTOR_BLOCKS * STATS_OUT
+        stats = keep.tile([P, vector_stats + X_CHUNKS * TRIPLE], F32)
         nc.vector.memset(stats[:, vector_stats:], float(SCALAR_COLS))
         part_sum = keep.tile([P, X_CHUNKS], F32)
         neg_mean = keep.tile([P, X_CHUNKS], F32)
@@ -158,11 +169,11 @@ def tile_vit_transformerblock_pa_k_kernel(
             for j in range(VECTOR_BLOCKS):
                 i = c * VECTOR_BLOCKS + j
                 nc.vector.bn_stats(
-                    out=stats[:, 6 * i : 6 * i + 6],
+                    out=stats[:, STATS_OUT * i : STATS_OUT * (i + 1)],
                     in_=x_tiles[c][:, j * STAT_COLS : (j + 1) * STAT_COLS],
                 )
             part = x_tiles[c][:, VECTOR_BLOCKS * STAT_COLS :]
-            triple = vector_stats + 3 * c
+            triple = vector_stats + TRIPLE * c
             nc.scalar.activation(
                 out=unused[:], in_=part, func=ACT.Copy, accum_out=part_sum[:, c : c + 1]
             )
@@ -190,7 +201,7 @@ def tile_vit_transformerblock_pa_k_kernel(
 
         xn_tiles = {}
         bank_tiles = {}
-        plane_tiles = {}
+        h_tiles = {}
         h_codes = {}
         h_scales = {}
         acc = [acc_pool.tile([P, E], F32, name="acc%d" % w) for w in range(N_W)]
@@ -201,7 +212,7 @@ def tile_vit_transformerblock_pa_k_kernel(
             xn = work.tile([P, G_ROUND, PACK, P], F32, name="xn", tag="xn")
             nc.vector.tensor_scalar(
                 out=xn[:],
-                in0=x_part.rearrange("r (g p t) -> r g t p", g=G_ROUND, t=PACK),
+                in0=x_part.rearrange("m (g p t) -> m g t p", g=G_ROUND, t=PACK),
                 scalar1=mean_var[:, 0:1],
                 scalar2=rstd[:, 0:1],
                 op0=ALU.subtract,
@@ -220,24 +231,22 @@ def tile_vit_transformerblock_pa_k_kernel(
                 bank_tiles[r].append(bank)
 
         def scale_and_shift(r):
-            h_planes = work.tile([P, G_ROUND, PACK, P], BF16, name="h_planes", tag="h_planes")
+            h_by_t = work.tile([P, G_ROUND, PACK, P], BF16, name="h_by_t", tag="h_by_t")
             for gi in range(G_ROUND):
                 g = r * G_ROUND + gi
                 for t in range(PACK):
                     nc.scalar.activation(
-                        out=h_planes[:, gi, t, :],
+                        out=h_by_t[:, gi, t, :],
                         in_=bank_tiles[r][gi][:, t, :],
                         func=ACT.Identity,
                         scale=gb[:, t, g : g + 1],
                         bias=gb[:, t, GROUPS + g : GROUPS + g + 1],
                     )
-            plane_tiles[r] = h_planes
+            h_tiles[r] = h_by_t
 
         def quantise(r):
             grouped = work.tile([P, G_ROUND, P, PACK], BF16, name="grouped", tag="grouped", align_bytes=64)
-            nc.vector.tensor_copy(
-                out=grouped[:], in_=plane_tiles[r][:].rearrange("p g t r -> p g r t")
-            )
+            nc.vector.tensor_copy(out=grouped[:], in_=h_tiles[r][:].rearrange("p g t m -> p g m t"))
             codes = h_pool.tile([P, G_ROUND * P], U32, name="codes", tag="codes", align_bytes=64)
             code_scales = h_pool.tile(
                 [P, G_ROUND * P], U8, name="code_scales", tag="code_scales", align_bytes=64
@@ -245,7 +254,7 @@ def tile_vit_transformerblock_pa_k_kernel(
             nc.vector.quantize_mx(
                 out=codes[:].bitcast(FP8X4),
                 scales=code_scales[:],
-                in_=grouped[:].rearrange("p g r t -> p (g r t)"),
+                in_=grouped[:].rearrange("p g m t -> p (g m t)"),
             )
             h_codes[r] = codes
             h_scales[r] = code_scales
@@ -259,7 +268,7 @@ def tile_vit_transformerblock_pa_k_kernel(
                         lhsT=h_codes[r][:, gi * P : (gi + 1) * P].bitcast(FP8X4),
                         lhsT_scale=h_scales[r][:, gi * P : (gi + 1) * P],
                         rhs=w_tiles[(r, w)][:, gi, :].bitcast(FP8X4),
-                        rhs_scale=planes[g // G_PLANES][PACK * w : P, g % G_PLANES, :],
+                        rhs_scale=planes[PACK * w : P, g, :],
                         start=(g == 0),
                         stop=(g == GROUPS - 1),
                     )
@@ -271,10 +280,10 @@ def tile_vit_transformerblock_pa_k_kernel(
         def finish(w):
             result = out_pool.tile([P, E], F32, name="result", tag="result")
             nc.vector.tensor_tensor(out=result[:], in0=acc[w][:], in1=bias_all[:, w, :], op=ALU.add)
-            for b in range(2):
+            for b in range(BATCH):
                 nc.sync.dma_start(
                     out=outs[w][b].rearrange("a n d -> n a d"),
-                    in_=result[b * 64 : (b + 1) * 64, :].rearrange("n (a d) -> n a d", a=HEADS),
+                    in_=result[b * TOKENS : (b + 1) * TOKENS, :].rearrange("n (a d) -> n a d", a=HEADS),
                 )
 
         normalise(0)

@@ -81,8 +81,24 @@ def tile_vit_transformerblock_pa_k_kernel(
         t_pool = ctx.enter_context(tc.psum_pool(name="t_pool", bufs=T_BANKS))
         ctx.enter_context(tc.manual_schedule())
 
+        gb_rows = keep.tile([P, K_PASS], BF16)
+        nc.vector.memset(gb_rows[:], 0.0)
+        nc.scalar.dma_start(out=gb_rows[0:GROUPS, :], in_=gamma.rearrange("(g k) -> g k", k=K_PASS))
+        nc.scalar.dma_start(
+            out=gb_rows[GROUPS : 2 * GROUPS, :], in_=beta.rearrange("(g k) -> g k", k=K_PASS)
+        )
+        bias_rows = keep.tile([P, N_W, E], BF16)
+        nc.vector.memset(bias_rows[:], 0.0)
+        for w in range(N_W):
+            nc.scalar.dma_start(
+                out=bias_rows[0:1, w, :], in_=biases[w].rearrange("(o e) -> o e", o=1)
+            )
+
+        ident = keep.tile([P, P], F32)
+        make_identity(nc, ident[:])
+
         planes = keep.tile([P, GROUPS, E], U8, align_bytes=64)
-        nc.vector.memset(planes[:].rearrange("p g n -> p (g n)").bitcast(I32), 0)
+        nc.gpsimd.memset(planes[:].rearrange("p g n -> p (g n)").bitcast(I32), 0)
 
         def load_scales(i):
             s, low = divmod(i, 2)
@@ -119,24 +135,9 @@ def tile_vit_transformerblock_pa_k_kernel(
                 load_x(i)
             else:
                 load_weights(i - X_CHUNKS)
-            if 1 <= i <= SCALE_BATCHES:
-                load_scales(i - 1)
+            if X_CHUNKS <= i < X_CHUNKS + SCALE_BATCHES:
+                load_scales(i - X_CHUNKS)
 
-        gb_rows = keep.tile([P, K_PASS], BF16)
-        nc.vector.memset(gb_rows[:], 0.0)
-        nc.scalar.dma_start(out=gb_rows[0:GROUPS, :], in_=gamma.rearrange("(g k) -> g k", k=K_PASS))
-        nc.scalar.dma_start(
-            out=gb_rows[GROUPS : 2 * GROUPS, :], in_=beta.rearrange("(g k) -> g k", k=K_PASS)
-        )
-        bias_rows = keep.tile([P, N_W, E], BF16)
-        nc.vector.memset(bias_rows[:], 0.0)
-        for w in range(N_W):
-            nc.scalar.dma_start(
-                out=bias_rows[0:1, w, :], in_=biases[w].rearrange("(o e) -> o e", o=1)
-            )
-
-        ident = keep.tile([P, P], F32)
-        make_identity(nc, ident[:])
         ones = keep.tile([P, P], BF16)
         nc.vector.memset(ones[:], 1.0)
         warm = keep.tile([P, 1], F32)

@@ -36,6 +36,8 @@ SCALAR_COLS = X_COLS - VECTOR_BLOCKS * STAT_COLS
 G_ROUND = 4
 ROUNDS = GROUPS // G_ROUND
 W_BUFS = 12
+FINE_FROM = 3
+FINE_GROUPS = 2
 T_BANKS = 5
 SCALE_BATCH = 2 * N_W
 SCALE_BATCHES = N_W * SCALE_ROWS // SCALE_BATCH
@@ -124,10 +126,13 @@ def tile_vit_transformerblock_pa_k_kernel(
         def load_weights(i):
             r, w = loads[i]
             w_chunk = w_pool.tile([P, G_ROUND, E], U32, name="w_chunk", tag="w_chunk", align_bytes=64)
-            nc.sync.dma_start(
-                out=w_chunk[:].bitcast(I32),
-                in_=words[w][:, r * G_ROUND : (r + 1) * G_ROUND, :].bitcast(I32),
-            )
+            step = G_ROUND if r < FINE_FROM else FINE_GROUPS
+            for gi in range(0, G_ROUND, step):
+                g = r * G_ROUND + gi
+                nc.sync.dma_start(
+                    out=w_chunk[:, gi : gi + step, :].bitcast(I32),
+                    in_=words[w][:, g : g + step, :].bitcast(I32),
+                )
             w_tiles[(r, w)] = w_chunk
 
         for i in range(X_CHUNKS + W_BUFS):

@@ -35,6 +35,7 @@ VECTOR_BLOCKS = 6
 SCALAR_COLS = X_COLS - VECTOR_BLOCKS * STAT_COLS
 G_ROUND = 4
 ROUNDS = GROUPS // G_ROUND
+LAG = 3
 W_BUFS = 12
 FINE_FROM = 3
 FINE_GROUPS = 2
@@ -150,20 +151,25 @@ def tile_vit_transformerblock_pa_k_kernel(
         nc.scalar.activation(out=warm[:], in_=warm[:], func=ACT.Sqrt)
 
         gb_sorted = keep.tile([P, PACK, P], F32)
-        nc.scalar.copy(out=gb_sorted[:], in_=gb_rows[:].rearrange("m (p t) -> m t p", t=PACK))
-        gb_bank = t_pool.tile([P, PACK, P], F32, name="gb_bank", tag="bank")
-        for t in range(PACK):
-            nc.tensor.transpose(out=gb_bank[:, t, :], in_=gb_sorted[:, t, :], identity=ident[:])
+        nc.gpsimd.tensor_copy(out=gb_sorted[:], in_=gb_rows[:].rearrange("m (p t) -> m t p", t=PACK))
         gb = keep.tile([P, PACK, P], F32)
-        nc.scalar.copy(out=gb[:], in_=gb_bank[:])
 
         bias_all = keep.tile([P, N_W, E], F32)
+        bias_banks = []
         for w in range(N_W):
             bias_bank = t_pool.tile([P, E], F32, name="bias_bank", tag="bank")
             nc.tensor.matmul(
                 out=bias_bank[:], lhsT=ones[:], rhs=bias_rows[:, w, :], start=True, stop=True
             )
-            nc.scalar.copy(out=bias_all[:, w, :], in_=bias_bank[:])
+            bias_banks.append(bias_bank)
+        gb_bank = t_pool.tile([P, PACK, P], F32, name="gb_bank", tag="bank")
+        for t in range(PACK):
+            nc.tensor.transpose(out=gb_bank[:, t, :], in_=gb_sorted[:, t, :], identity=ident[:])
+
+        constant_copies = {
+            1: [(bias_all[:, 0, :], bias_banks[0]), (bias_all[:, 1, :], bias_banks[1])],
+            2: [(bias_all[:, 2, :], bias_banks[2]), (gb[:], gb_bank)],
+        }
 
         vector_stats = X_CHUNKS * VECTOR_BLOCKS * STATS_OUT
         stats = keep.tile([P, vector_stats + X_CHUNKS * TRIPLE], F32)
@@ -194,6 +200,8 @@ def tile_vit_transformerblock_pa_k_kernel(
                 bias=neg_mean[:, c : c + 1],
                 accum_out=stats[:, triple + 2 : triple + 3],
             )
+            for out, bank in constant_copies.get(c, []):
+                nc.scalar.copy(out=out, in_=bank[:])
         mean_var = keep.tile([P, 2], F32)
         nc.vector.bn_aggr(out=mean_var[:], in_=stats[:])
         var_eps = keep.tile([P, 1], F32)
@@ -302,6 +310,7 @@ def tile_vit_transformerblock_pa_k_kernel(
             if r + 2 < ROUNDS:
                 normalise(r + 2)
             quantise(r)
-            if r >= 1:
-                multiply(r - 1)
-        multiply(ROUNDS - 1)
+            if r >= LAG:
+                multiply(r - LAG)
+        for r in range(ROUNDS - LAG, ROUNDS):
+            multiply(r)

@@ -17,7 +17,7 @@ BATCH = 2
 TOKENS = 64
 D = 16384
 E = 512
-HEADS = 8
+HEAD_DIM = 64
 EPS = 1e-5
 PACK = 4
 K_PASS = P * PACK
@@ -39,7 +39,8 @@ LAG = 3
 W_BUFS = 12
 FINE_FROM = 3
 FINE_GROUPS = 2
-T_BANKS = 5
+V_COLS = E // 2
+T_BANKS = 4
 SCALE_BATCH = 2 * N_W
 SCALE_BATCHES = N_W * SCALE_ROWS // SCALE_BATCH
 
@@ -79,7 +80,7 @@ def tile_vit_transformerblock_pa_k_kernel(
         w_pool = ctx.enter_context(tc.tile_pool(name="w_pool", bufs=W_BUFS))
         work = ctx.enter_context(tc.tile_pool(name="work", bufs=2))
         h_pool = ctx.enter_context(tc.tile_pool(name="h_pool", bufs=ROUNDS))
-        out_pool = ctx.enter_context(tc.tile_pool(name="out_pool", bufs=N_W))
+        out_pool = ctx.enter_context(tc.tile_pool(name="out_pool", bufs=N_W + 1))
         acc_pool = ctx.enter_context(tc.psum_pool(name="acc_pool", bufs=1))
         t_pool = ctx.enter_context(tc.psum_pool(name="t_pool", bufs=T_BANKS))
         ctx.enter_context(tc.manual_schedule())
@@ -128,11 +129,15 @@ def tile_vit_transformerblock_pa_k_kernel(
             r, w = loads[i]
             w_chunk = w_pool.tile([P, G_ROUND, E], U32, name="w_chunk", tag="w_chunk", align_bytes=64)
             step = G_ROUND if r < FINE_FROM else FINE_GROUPS
-            for gi in range(0, G_ROUND, step):
+            pieces = [(gi, step, 0, E) for gi in range(0, G_ROUND, step)]
+            if i == len(loads) - 1:
+                gi = pieces.pop(len(pieces) - 1)[0]
+                pieces.extend([(gi, step, col, V_COLS) for col in range(0, E, V_COLS)])
+            for gi, count, col, cols in pieces:
                 g = r * G_ROUND + gi
                 nc.sync.dma_start(
-                    out=w_chunk[:, gi : gi + step, :].bitcast(I32),
-                    in_=words[w][:, g : g + step, :].bitcast(I32),
+                    out=w_chunk[:, gi : gi + count, col : col + cols].bitcast(I32),
+                    in_=words[w][:, g : g + count, PACK * col : PACK * (col + cols)].bitcast(I32),
                 )
             w_tiles[(r, w)] = w_chunk
 
@@ -218,7 +223,8 @@ def tile_vit_transformerblock_pa_k_kernel(
         h_tiles = {}
         h_codes = {}
         h_scales = {}
-        acc = [acc_pool.tile([P, E], F32, name="acc%d" % w) for w in range(N_W)]
+        parts = [(0, 0, E), (1, 0, E), (2, 0, V_COLS), (2, V_COLS, V_COLS)]
+        acc = [acc_pool.tile([P, E], F32, name="acc%d" % i) for i in range(len(parts))]
 
         def normalise(r):
             c, j = divmod(r, X_COLS // (G_ROUND * K_PASS))
@@ -273,31 +279,47 @@ def tile_vit_transformerblock_pa_k_kernel(
             h_codes[r] = codes
             h_scales[r] = code_scales
 
+        def one_pass(r, gi, part):
+            w, col, cols = parts[part]
+            g = r * G_ROUND + gi
+            nc.tensor.matmul_mx(
+                out=acc[part][:, :cols],
+                lhsT=h_codes[r][:, gi * P : (gi + 1) * P].bitcast(FP8X4),
+                lhsT_scale=h_scales[r][:, gi * P : (gi + 1) * P],
+                rhs=w_tiles[(r, w)][:, gi, col : col + cols].bitcast(FP8X4),
+                rhs_scale=planes[PACK * w : P, g, col : col + cols],
+                start=(g == 0),
+                stop=(g == GROUPS - 1),
+            )
+
         def multiply(r):
             for w in range(N_W):
-                for gi in range(G_ROUND):
-                    g = r * G_ROUND + gi
-                    nc.tensor.matmul_mx(
-                        out=acc[w][:],
-                        lhsT=h_codes[r][:, gi * P : (gi + 1) * P].bitcast(FP8X4),
-                        lhsT_scale=h_scales[r][:, gi * P : (gi + 1) * P],
-                        rhs=w_tiles[(r, w)][:, gi, :].bitcast(FP8X4),
-                        rhs_scale=planes[PACK * w : P, g, :],
-                        start=(g == 0),
-                        stop=(g == GROUPS - 1),
-                    )
+                own_parts = [i for i in range(len(parts)) if parts[i][0] == w]
+                for part in own_parts:
+                    for gi in range(G_ROUND):
+                        one_pass(r, gi, part)
+                    if r == ROUNDS - 1:
+                        finish(part)
                 if r * N_W + w + W_BUFS < len(loads):
                     load_weights(r * N_W + w + W_BUFS)
-                if r == ROUNDS - 1:
-                    finish(w)
 
-        def finish(w):
+        def finish(part):
+            w, col, cols = parts[part]
+            heads = slice(col // HEAD_DIM, (col + cols) // HEAD_DIM)
             result = out_pool.tile([P, E], F32, name="result", tag="result")
-            nc.vector.tensor_tensor(out=result[:], in0=acc[w][:], in1=bias_all[:, w, :], op=ALU.add)
+            nc.vector.tensor_tensor(
+                out=result[:, :cols],
+                in0=acc[part][:, :cols],
+                in1=bias_all[:, w, col : col + cols],
+                op=ALU.add,
+            )
             for b in range(BATCH):
-                nc.sync.dma_start(
-                    out=outs[w][b].rearrange("a n d -> n a d"),
-                    in_=result[b * TOKENS : (b + 1) * TOKENS, :].rearrange("n (a d) -> n a d", a=HEADS),
+                queue = nc.scalar if part == len(parts) - 1 and b == BATCH - 1 else nc.sync
+                queue.dma_start(
+                    out=outs[w][b][heads].rearrange("a n d -> n a d"),
+                    in_=result[b * TOKENS : (b + 1) * TOKENS, :cols].rearrange(
+                        "n (a d) -> n a d", d=HEAD_DIM
+                    ),
                 )
 
         normalise(0)

from contextlib import ExitStack

import concourse.mybir as mybir
from concourse.masks import make_identity

F32 = mybir.dt.float32
BF16 = mybir.dt.bfloat16
I32 = mybir.dt.int32
U32 = mybir.dt.uint32
U8 = mybir.dt.uint8
FP8X4 = mybir.dt.float8_e4m3fn_x4
ALU = mybir.AluOpType
ACT = mybir.ActivationFunctionType

P = 128
BATCH = 2
TOKENS = 64
D = 16384
E = 512
HEAD_DIM = 64
EPS = 1e-5
PACK = 4
K_PASS = P * PACK
GROUPS = D // K_PASS
N_W = 3
SCALE_ROWS = K_PASS // 32
QUADRANT = 32

X_CHUNKS = 4
X_COLS = D // X_CHUNKS
STAT_COLS = 512
STATS_OUT = 6
TRIPLE = 3
VECTOR_BLOCKS = 6
SCALAR_COLS = X_COLS - VECTOR_BLOCKS * STAT_COLS
G_ROUND = 4
ROUNDS = GROUPS // G_ROUND
LAG = 3
W_BUFS = 12
FINE_FROM = 3
FINE_GROUPS = 2
V_COLS = E // 2
T_BANKS = 4
SCALE_BATCH = 2 * N_W
SCALE_BATCHES = N_W * SCALE_ROWS // SCALE_BATCH

FLOPS = 2 * P * D * N_W * E


def tile_vit_transformerblock_pa_k_kernel(
    tc,
    x,
    gamma,
    beta,
    Wq_words,
    Wq_scales,
    bq,
    Wk_words,
    Wk_scales,
    bk,
    Wv_words,
    Wv_scales,
    bv,
    out_0,
    out_1,
    out_2,
):
    nc = tc.nc
    x_rows = x.rearrange("b n d -> (b n) d")
    words = [
        packed.rearrange("g p n t -> p g (n t)") for packed in (Wq_words, Wk_words, Wv_words)
    ]
    scales = [Wq_scales, Wk_scales, Wv_scales]
    biases = [bq, bk, bv]
    outs = [out_0, out_1, out_2]

    with ExitStack() as ctx:
        keep = ctx.enter_context(tc.tile_pool(name="keep", bufs=1))
        x_pool = ctx.enter_context(tc.tile_pool(name="x_pool", bufs=X_CHUNKS))
        w_pool = ctx.enter_context(tc.tile_pool(name="w_pool", bufs=W_BUFS))
        work = ctx.enter_context(tc.tile_pool(name="work", bufs=2))
        h_pool = ctx.enter_context(tc.tile_pool(name="h_pool", bufs=ROUNDS))
        out_pool = ctx.enter_context(tc.tile_pool(name="out_pool", bufs=N_W + 1))
        acc_pool = ctx.enter_context(tc.psum_pool(name="acc_pool", bufs=1))
        t_pool = ctx.enter_context(tc.psum_pool(name="t_pool", bufs=T_BANKS))
        ctx.enter_context(tc.manual_schedule())

        gb_rows = keep.tile([P, K_PASS], BF16)
        nc.vector.memset(gb_rows[:], 0.0)
        nc.scalar.dma_start(out=gb_rows[0:GROUPS, :], in_=gamma.rearrange("(g k) -> g k", k=K_PASS))
        nc.scalar.dma_start(
            out=gb_rows[GROUPS : 2 * GROUPS, :], in_=beta.rearrange("(g k) -> g k", k=K_PASS)
        )
        bias_rows = keep.tile([P, N_W, E], BF16)
        nc.vector.memset(bias_rows[:], 0.0)
        for w in range(N_W):
            nc.scalar.dma_start(
                out=bias_rows[0:1, w, :], in_=biases[w].rearrange("(o e) -> o e", o=1)
            )

        ident = keep.tile([P, P], F32)
        make_identity(nc, ident[:])

        planes = keep.tile([P, GROUPS, E], U8, align_bytes=64)
        nc.gpsimd.memset(planes[:].rearrange("p g n -> p (g n)").bitcast(I32), 0)

        def load_scales(i):
            s, low = divmod(i, 2)
            for high in range(2):
                for w in range(N_W):
                    q = PACK * (2 * high + low) + s
                    row = QUADRANT * (2 * high + low) + PACK * w + s
                    nc.sync.dma_start(
                        out=planes[row : row + 1, :, :].bitcast(I32),
                        in_=scales[w][:, q : q + 1, :].rearrange("g o n -> o g n").bitcast(I32),
                    )

        x_tiles = []

        def load_x(c):
            x_chunk = x_pool.tile([P, X_COLS], BF16, name="x_chunk", tag="x_chunk")
            nc.sync.dma_start(out=x_chunk[:], in_=x_rows[:, c * X_COLS : (c + 1) * X_COLS])
            x_tiles.append(x_chunk)

        loads = [(r, w) for r in range(ROUNDS) for w in range(N_W)]
        w_tiles = {}

        def load_weights(i):
            r, w = loads[i]
            w_chunk = w_pool.tile([P, G_ROUND, E], U32, name="w_chunk", tag="w_chunk", align_bytes=64)
            step = G_ROUND if r < FINE_FROM else FINE_GROUPS
            pieces = [(gi, step, 0, E) for gi in range(0, G_ROUND, step)]
            if i == len(loads) - 1:
                gi = pieces.pop(len(pieces) - 1)[0]
                pieces.extend([(gi, step, col, V_COLS) for col in range(0, E, V_COLS)])
            for gi, count, col, cols in pieces:
                g = r * G_ROUND + gi
                nc.sync.dma_start(
                    out=w_chunk[:, gi : gi + count, col : col + cols].bitcast(I32),
                    in_=words[w][:, g : g + count, PACK * col : PACK * (col + cols)].bitcast(I32),
                )
            w_tiles[(r, w)] = w_chunk

        for i in range(X_CHUNKS + W_BUFS):
            if i < X_CHUNKS:
                load_x(i)
            else:
                load_weights(i - X_CHUNKS)
            if X_CHUNKS <= i < X_CHUNKS + SCALE_BATCHES:
                load_scales(i - X_CHUNKS)

        ones = keep.tile([P, P], BF16)
        nc.vector.memset(ones[:], 1.0)
        warm = keep.tile([P, 1], F32)
        nc.vector.memset(warm[:], 1.0)
        nc.scalar.activation(out=warm[:], in_=warm[:], func=ACT.Sqrt)

        gb_sorted = keep.tile([P, PACK, P], F32)
        nc.gpsimd.tensor_copy(out=gb_sorted[:], in_=gb_rows[:].rearrange("m (p t) -> m t p", t=PACK))
        gb = keep.tile([P, PACK, P], F32)

        bias_all = keep.tile([P, N_W, E], F32)
        bias_banks = []
        for w in range(N_W):
            bias_bank = t_pool.tile([P, E], F32, name="bias_bank", tag="bank")
            nc.tensor.matmul(
                out=bias_bank[:], lhsT=ones[:], rhs=bias_rows[:, w, :], start=True, stop=True
            )
            bias_banks.append(bias_bank)
        gb_bank = t_pool.tile([P, PACK, P], F32, name="gb_bank", tag="bank")
        for t in range(PACK):
            nc.tensor.transpose(out=gb_bank[:, t, :], in_=gb_sorted[:, t, :], identity=ident[:])

        constant_copies = {
            1: [(bias_all[:, 0, :], bias_banks[0]), (bias_all[:, 1, :], bias_banks[1])],
            2: [(bias_all[:, 2, :], bias_banks[2]), (gb[:], gb_bank)],
        }

        vector_stats = X_CHUNKS * VECTOR_BLOCKS * STATS_OUT
        stats = keep.tile([P, vector_stats + X_CHUNKS * TRIPLE], F32)
        nc.vector.memset(stats[:, vector_stats:], float(SCALAR_COLS))
        part_sum = keep.tile([P, X_CHUNKS], F32)
        neg_mean = keep.tile([P, X_CHUNKS], F32)
        unused = keep.tile([P, SCALAR_COLS], BF16)
        for c in range(X_CHUNKS):
            for j in range(VECTOR_BLOCKS):
                i = c * VECTOR_BLOCKS + j
                nc.vector.bn_stats(
                    out=stats[:, STATS_OUT * i : STATS_OUT * (i + 1)],
                    in_=x_tiles[c][:, j * STAT_COLS : (j + 1) * STAT_COLS],
                )
            part = x_tiles[c][:, VECTOR_BLOCKS * STAT_COLS :]
            triple = vector_stats + TRIPLE * c
            nc.scalar.activation(
                out=unused[:], in_=part, func=ACT.Copy, accum_out=part_sum[:, c : c + 1]
            )
            nc.scalar.mul(
                out=stats[:, triple + 1 : triple + 2], in_=part_sum[:, c : c + 1], mul=1.0 / SCALAR_COLS
            )
            nc.scalar.mul(out=neg_mean[:, c : c + 1], in_=part_sum[:, c : c + 1], mul=-1.0 / SCALAR_COLS)
            nc.scalar.activation(
                out=unused[:],
                in_=part,
                func=ACT.Square,
                bias=neg_mean[:, c : c + 1],
                accum_out=stats[:, triple + 2 : triple + 3],
            )
            for out, bank in constant_copies.get(c, []):
                nc.scalar.copy(out=out, in_=bank[:])
        mean_var = keep.tile([P, 2], F32)
        nc.vector.bn_aggr(out=mean_var[:], in_=stats[:])
        var_eps = keep.tile([P, 1], F32)
        nc.vector.tensor_scalar(
            out=var_eps[:], in0=mean_var[:, 1:2], scalar1=EPS, scalar2=None, op0=ALU.add
        )
        std = keep.tile([P, 1], F32)
        nc.scalar.activation(out=std[:], in_=var_eps[:], func=ACT.Sqrt)
        rstd = keep.tile([P, 1], F32)
        nc.vector.reciprocal(out=rstd[:], in_=std[:])

        xn_tiles = {}
        bank_tiles = {}
        h_tiles = {}
        h_codes = {}
        h_scales = {}
        parts = [(0, 0, E), (1, 0, E), (2, 0, V_COLS), (2, V_COLS, V_COLS)]
        acc = [acc_pool.tile([P, E], F32, name="acc%d" % i) for i in range(len(parts))]

        def normalise(r):
            c, j = divmod(r, X_COLS // (G_ROUND * K_PASS))
            x_part = x_tiles[c][:, j * G_ROUND * K_PASS : (j + 1) * G_ROUND * K_PASS]
            xn = work.tile([P, G_ROUND, PACK, P], F32, name="xn", tag="xn")
            nc.vector.tensor_scalar(
                out=xn[:],
                in0=x_part.rearrange("m (g p t) -> m g t p", g=G_ROUND, t=PACK),
                scalar1=mean_var[:, 0:1],
                scalar2=rstd[:, 0:1],
                op0=ALU.subtract,
                op1=ALU.mult,
            )
            xn_tiles[r] = xn

        def transpose(r):
            bank_tiles[r] = []
            for gi in range(G_ROUND):
                bank = t_pool.tile([P, PACK, P], F32, name="bank", tag="bank")
                for t in range(PACK):
                    nc.tensor.transpose(
                        out=bank[:, t, :], in_=xn_tiles[r][:, gi, t, :], identity=ident[:]
                    )
                bank_tiles[r].append(bank)

        def scale_and_shift(r):
            h_by_t = work.tile([P, G_ROUND, PACK, P], BF16, name="h_by_t", tag="h_by_t")
            for gi in range(G_ROUND):
                g = r * G_ROUND + gi
                for t in range(PACK):
                    nc.scalar.activation(
                        out=h_by_t[:, gi, t, :],
                        in_=bank_tiles[r][gi][:, t, :],
                        func=ACT.Identity,
                        scale=gb[:, t, g : g + 1],
                        bias=gb[:, t, GROUPS + g : GROUPS + g + 1],
                    )
            h_tiles[r] = h_by_t

        def quantise(r):
            grouped = work.tile([P, G_ROUND, P, PACK], BF16, name="grouped", tag="grouped", align_bytes=64)
            nc.vector.tensor_copy(out=grouped[:], in_=h_tiles[r][:].rearrange("p g t m -> p g m t"))
            codes = h_pool.tile([P, G_ROUND * P], U32, name="codes", tag="codes", align_bytes=64)
            code_scales = h_pool.tile(
                [P, G_ROUND * P], U8, name="code_scales", tag="code_scales", align_bytes=64
            )
            nc.vector.quantize_mx(
                out=codes[:].bitcast(FP8X4),
                scales=code_scales[:],
                in_=grouped[:].rearrange("p g m t -> p (g m t)"),
            )
            h_codes[r] = codes
            h_scales[r] = code_scales

        def one_pass(r, gi, part):
            w, col, cols = parts[part]
            g = r * G_ROUND + gi
            nc.tensor.matmul_mx(
                out=acc[part][:, :cols],
                lhsT=h_codes[r][:, gi * P : (gi + 1) * P].bitcast(FP8X4),
                lhsT_scale=h_scales[r][:, gi * P : (gi + 1) * P],
                rhs=w_tiles[(r, w)][:, gi, col : col + cols].bitcast(FP8X4),
                rhs_scale=planes[PACK * w : P, g, col : col + cols],
                start=(g == 0),
                stop=(g == GROUPS - 1),
            )

        def multiply(r):
            for w in range(N_W):
                own_parts = [i for i in range(len(parts)) if parts[i][0] == w]
                for part in own_parts:
                    for gi in range(G_ROUND):
                        one_pass(r, gi, part)
                    if r == ROUNDS - 1:
                        finish(part)
                if r * N_W + w + W_BUFS < len(loads):
                    load_weights(r * N_W + w + W_BUFS)

        def finish(part):
            w, col, cols = parts[part]
            heads = slice(col // HEAD_DIM, (col + cols) // HEAD_DIM)
            result = out_pool.tile([P, E], F32, name="result", tag="result")
            nc.vector.tensor_tensor(
                out=result[:, :cols],
                in0=acc[part][:, :cols],
                in1=bias_all[:, w, col : col + cols],
                op=ALU.add,
            )
            for b in range(BATCH):
                queue = nc.scalar if part == len(parts) - 1 and b == BATCH - 1 else nc.sync
                queue.dma_start(
                    out=outs[w][b][heads].rearrange("a n d -> n a d"),
                    in_=result[b * TOKENS : (b + 1) * TOKENS, :cols].rearrange(
                        "n (a d) -> n a d", d=HEAD_DIM
                    ),
                )

        normalise(0)
        transpose(0)
        normalise(1)
        for r in range(ROUNDS):
            scale_and_shift(r)
            if r + 1 < ROUNDS:
                transpose(r + 1)
            if r + 2 < ROUNDS:
                normalise(r + 2)
            quantise(r)
            if r >= LAG:
                multiply(r - LAG)
        for r in range(ROUNDS - LAG, ROUNDS):
            multiply(r)
